import numpy as np
import ml_dtypes


def mxq(x, axis, fmt="e4m3"):
    dtype, down = {"e4m3": (ml_dtypes.float8_e4m3fn, 7), "e5m2": (ml_dtypes.float8_e5m2, 14)}[fmt]
    v = np.moveaxis(np.asarray(x, np.float32).astype(ml_dtypes.bfloat16).astype(np.float64), axis, -1)
    blocks = v.reshape(v.shape[:-1] + (-1, 32))
    amax = np.abs(blocks).max(-1, keepdims=True)
    byte = np.maximum(np.where(amax > 0, np.frexp(amax)[1] - 1 + 127, 0) - down, 1)
    scale = np.exp2(byte - 127.0)
    codes = (blocks / scale).astype(np.float32).astype(dtype).astype(np.float64)
    return np.moveaxis((codes * scale).reshape(v.shape), -1, axis)


WIDE = False


def mx_kscale(k):
    if not WIDE:
        return np.ones(k)
    levels = np.array([10, -10, 5, -5, 0])
    a = np.random.permutation(np.resize(levels, k // 512 * 4)).reshape(k // 512, 4)
    idx = np.arange(k)
    return np.exp2(a[idx // 512, idx % 128 // 32])


BF16 = ml_dtypes.bfloat16


def bf(x):
    return np.asarray(x, np.float32).astype(BF16)


def f64(x):
    return np.asarray(x).astype(np.float64)


B, N, D = 1, 128, 1024
P0 = 0.2


def setup_inputs():
    s = mx_kscale(D)
    g = 0.4 + 1.2 * np.random.random_sample((B, 1, N))
    bound = np.sqrt(6.0 / (D + D))
    return {"embedding": bf(np.random.standard_normal((B, D, N)) * g * np.sqrt(P0) / D ** 0.25 * s[None, :, None]),
            "heatm": bf(np.random.standard_normal((B, D, N))),
            "W_b": bf(np.random.uniform(-bound, bound, (D, D)) / s[:, None] / s[None, :])}


def reference(embedding, heatm, W_b):
    eq = mxq(f64(embedding), 1, "e4m3")
    t = np.swapaxes(eq, 1, 2) @ mxq(f64(W_b), 0, "e4m3")
    C = np.tanh(mxq(t, 2, "e4m3") @ eq)
    max_cow = np.max(C, axis=-1, keepdims=True)
    e = np.exp(max_cow - np.max(max_cow, axis=1, keepdims=True))
    return e / np.sum(e, axis=1, keepdims=True)

@@ -1,0 +1,136 @@
+from contextlib import ExitStack
+
+import concourse.mybir as mybir
+from concourse.masks import make_identity
+
+BF16 = mybir.dt.bfloat16
+F32 = mybir.dt.float32
+U32 = mybir.dt.uint32
+U8 = mybir.dt.uint8
+FP8X4 = mybir.dt.float8_e4m3fn_x4
+ACT = mybir.ActivationFunctionType
+ALU = mybir.AluOpType
+AXIS = mybir.AxisListType
+
+P = 128
+PACK = 4
+K_PASS = P * PACK
+D = 1024
+N = 128
+PASSES = D // K_PASS
+
+VECTOR_COLUMNS = 80
+
+FLOPS = 2 * N * D * D + 2 * N * N * D
+BYTES = 2 * D * N + 2 * D * D + 4 * N
+
+
+def tile_parallelcoattention_s_kernel(tc, embedding, heatm, W_b, out):
+    nc = tc.nc
+    with ExitStack() as ctx:
+        keep = ctx.enter_context(tc.tile_pool(name="keep", bufs=1))
+        stage = ctx.enter_context(tc.tile_pool(name="stage", bufs=PASSES * PASSES))
+        psum = ctx.enter_context(tc.psum_pool(name="psum", bufs=2))
+
+        e_raw = keep.tile([P, PASSES, PACK, N], BF16)
+        nc.sync.dma_start(
+            out=e_raw[:], in_=embedding[0].rearrange("(c p j) n -> p c j n", p=P, j=PACK)
+        )
+        w_rows = W_b.rearrange("(c p j) w -> c p j w", p=P, j=PACK)
+        w_raw = {}
+        for h in range(PASSES):
+            for c in range(PASSES):
+                w_raw[h, c] = stage.tile([P, PACK, K_PASS], BF16, name="w_raw")
+                nc.sync.dma_start(
+                    out=w_raw[h, c][:], in_=w_rows[c][:, :, h * K_PASS : (h + 1) * K_PASS]
+                )
+
+        zero = keep.tile([P, 1], F32)
+        nc.vector.memset(zero[:], 0.0)
+        warm = keep.tile([P, 1], F32)
+        nc.scalar.activation(out=warm[:], in_=zero[:], func=ACT.Tanh)
+        ident = keep.tile([P, P], F32)
+        make_identity(nc, ident[:])
+
+        e_grouped = keep.tile([P, PASSES, N, PACK], BF16, align_bytes=64)
+        nc.vector.tensor_copy(out=e_grouped[:], in_=e_raw[:].rearrange("p c j n -> p c n j"))
+        e_codes = keep.tile([P, PASSES, N], U32, align_bytes=64)
+        e_scales = keep.tile([P, PASSES, N], U8, align_bytes=64)
+        nc.vector.quantize_mx(
+            out=e_codes[:].rearrange("p c n -> p (c n)").bitcast(FP8X4),
+            scales=e_scales[:].rearrange("p c n -> p (c n)"),
+            in_=e_grouped[:].rearrange("p c n j -> p (c n j)"),
+        )
+
+        w_codes = keep.tile([P, PASSES, PASSES, PACK, P], U32, align_bytes=64)
+        w_scales = keep.tile([P, PASSES, PASSES, PACK, P], U8, align_bytes=64)
+        t_codes = keep.tile([P, PASSES, N], U32, align_bytes=64)
+        t_scales = keep.tile([P, PASSES, N], U8, align_bytes=64)
+        c_psum = psum.tile([P, N], F32)
+        for h in range(PASSES):
+            for c in range(PASSES):
+                w_grouped = stage.tile([P, PACK, P, PACK], BF16, align_bytes=64)
+                src = w_raw[h, c][:].rearrange("p j (q i) -> p q j i", i=PACK)
+                dst = w_grouped[:].rearrange("p i q j -> p q j i")
+                nc.vector.tensor_copy(
+                    out=dst[:, :VECTOR_COLUMNS], in_=src[:, :VECTOR_COLUMNS]
+                )
+                nc.scalar.copy(out=dst[:, VECTOR_COLUMNS:], in_=src[:, VECTOR_COLUMNS:])
+                nc.vector.quantize_mx(
+                    out=w_codes[:, h, c].rearrange("p i q -> p (i q)").bitcast(FP8X4),
+                    scales=w_scales[:, h, c].rearrange("p i q -> p (i q)"),
+                    in_=w_grouped[:].rearrange("p i q j -> p (i q j)"),
+                )
+
+            t_psum = psum.tile([P, PACK, N], F32)
+            for i in range(PACK):
+                for c in range(PASSES):
+                    nc.tensor.matmul_mx(
+                        out=t_psum[:, i, :],
+                        lhsT=w_codes[:, h, c, i, :].bitcast(FP8X4),
+                        lhsT_scale=w_scales[:, h, c, i, :],
+                        rhs=e_codes[:, c, :].bitcast(FP8X4),
+                        rhs_scale=e_scales[:, c, :],
+                        start=(c == 0),
+                        stop=(c == PASSES - 1),
+                    )
+
+            t_grouped = stage.tile([P, N, PACK], BF16, align_bytes=64)
+            nc.scalar.copy(out=t_grouped[:], in_=t_psum[:].rearrange("q i n -> q n i"))
+            nc.vector.quantize_mx(
+                out=t_codes[:, h, :].bitcast(FP8X4),
+                scales=t_scales[:, h, :],
+                in_=t_grouped[:].rearrange("q n i -> q (n i)"),
+            )
+            nc.tensor.matmul_mx(
+                out=c_psum[:],
+                lhsT=t_codes[:, h, :].bitcast(FP8X4),
+                lhsT_scale=t_scales[:, h, :],
+                rhs=e_codes[:, h, :].bitcast(FP8X4),
+                rhs_scale=e_scales[:, h, :],
+                start=(h == 0),
+                stop=(h == PASSES - 1),
+            )
+
+        row_max = keep.tile([P, 1], F32)
+        nc.vector.tensor_reduce(out=row_max[:], in_=c_psum[:], axis=AXIS.X, op=ALU.max)
+        m = keep.tile([P, 1], F32)
+        nc.scalar.activation(out=m[:], in_=row_max[:], func=ACT.Tanh)
+
+        m_rows = psum.tile([P, N], F32)
+        nc.tensor.transpose(m_rows[:], m[:, 0:1].to_broadcast([P, P]), ident[:])
+        minus_top = keep.tile([P, 1], F32)
+        nc.vector.tensor_reduce(
+            out=minus_top[:], in_=m_rows[:], axis=AXIS.X, op=ALU.max, negate=True
+        )
+        e = keep.tile([P, N], F32)
+        total = keep.tile([P, 1], F32)
+        nc.scalar.activation(
+            out=e[:], in_=m_rows[:], func=ACT.Exp, bias=minus_top[:], accum_out=total[:]
+        )
+        inverse = keep.tile([P, 1], F32)
+        nc.vector.reciprocal(out=inverse[:], in_=total[:])
+        weights = keep.tile([P, N], F32)
+        nc.vector.tensor_scalar_mul(out=weights[:], in0=e[:], scalar1=inverse[:])
+
+        nc.sync.dma_start(out=out.rearrange("b n o -> b (n o)"), in_=weights[0:1, :])

@@ -18,31 +18,52 @@ K_PASS = P * PACK
 D = 1024
 N = 128
 PASSES = D // K_PASS
+RUN = 4
 
-VECTOR_COLUMNS = 80
+END_PIECES = 2
+
+VECTOR_SIXTEENTHS = 9
 
 FLOPS = 2 * N * D * D + 2 * N * N * D
 BYTES = 2 * D * N + 2 * D * D + 4 * N
 
 
+def regroup(nc, grouped, raw):
+    src = raw.rearrange("p t (c i) -> p c t i", i=RUN)
+    dst = grouped.rearrange("p (c i) t -> p c t i", i=RUN)
+    split = src.shape[1] * VECTOR_SIXTEENTHS // 16
+    nc.vector.tensor_copy(out=dst[:, :split], in_=src[:, :split])
+    nc.scalar.copy(out=dst[:, split:], in_=src[:, split:])
+
+
 def tile_parallelcoattention_s_kernel(tc, embedding, heatm, W_b, out):
     nc = tc.nc
+
+    pieces = []
+    for h in range(PASSES):
+        for g in range(PASSES):
+            at_an_end = h == g and h in (0, PASSES - 1)
+            tiles = PACK // END_PIECES if at_an_end else PACK
+            for first in range(0, PACK, tiles):
+                pieces.append((h, g, first, tiles))
+
     with ExitStack() as ctx:
         keep = ctx.enter_context(tc.tile_pool(name="keep", bufs=1))
-        stage = ctx.enter_context(tc.tile_pool(name="stage", bufs=PASSES * PASSES))
+        stage = ctx.enter_context(tc.tile_pool(name="stage", bufs=len(pieces)))
         psum = ctx.enter_context(tc.psum_pool(name="psum", bufs=2))
 
         e_raw = keep.tile([P, PASSES, PACK, N], BF16)
-        nc.sync.dma_start(
-            out=e_raw[:], in_=embedding[0].rearrange("(c p j) n -> p c j n", p=P, j=PACK)
-        )
-        w_rows = W_b.rearrange("(c p j) w -> c p j w", p=P, j=PACK)
-        w_raw = {}
-        for h in range(PASSES):
-            for c in range(PASSES):
-                w_raw[h, c] = stage.tile([P, PACK, K_PASS], BF16, name="w_raw")
+        w_rows = W_b.rearrange("(g t p) w -> g p t w", t=PACK, p=P)
+        w_raw = []
+        for h, g, first, tiles in pieces:
+            raw = stage.tile([P, PACK, tiles * P], BF16, name="w_raw")
+            start = h * K_PASS + first * P
+            nc.sync.dma_start(out=raw[:], in_=w_rows[g][:, :, start : start + tiles * P])
+            w_raw.append(raw)
+            if h == 0 and g == 0 and first + tiles == PACK:
                 nc.sync.dma_start(
-                    out=w_raw[h, c][:], in_=w_rows[c][:, :, h * K_PASS : (h + 1) * K_PASS]
+                    out=e_raw[:],
+                    in_=embedding[0].rearrange("(g t p) n -> p g t n", t=PACK, p=P),
                 )
 
         zero = keep.tile([P, 1], F32)
@@ -52,51 +73,19 @@ def tile_parallelcoattention_s_kernel(tc, embedding, heatm, W_b, out):
         ident = keep.tile([P, P], F32)
         make_identity(nc, ident[:])
 
-        e_grouped = keep.tile([P, PASSES, N, PACK], BF16, align_bytes=64)
-        nc.vector.tensor_copy(out=e_grouped[:], in_=e_raw[:].rearrange("p c j n -> p c n j"))
-        e_codes = keep.tile([P, PASSES, N], U32, align_bytes=64)
-        e_scales = keep.tile([P, PASSES, N], U8, align_bytes=64)
-        nc.vector.quantize_mx(
-            out=e_codes[:].rearrange("p c n -> p (c n)").bitcast(FP8X4),
-            scales=e_scales[:].rearrange("p c n -> p (c n)"),
-            in_=e_grouped[:].rearrange("p c n j -> p (c n j)"),
-        )
-
         w_codes = keep.tile([P, PASSES, PASSES, PACK, P], U32, align_bytes=64)
         w_scales = keep.tile([P, PASSES, PASSES, PACK, P], U8, align_bytes=64)
         t_codes = keep.tile([P, PASSES, N], U32, align_bytes=64)
         t_scales = keep.tile([P, PASSES, N], U8, align_bytes=64)
+        e_grouped = keep.tile([P, PASSES, N, PACK], BF16, align_bytes=64)
+        e_codes = keep.tile([P, PASSES, N], U32, align_bytes=64)
+        e_scales = keep.tile([P, PASSES, N], U8, align_bytes=64)
         c_psum = psum.tile([P, N], F32)
-        for h in range(PASSES):
-            for c in range(PASSES):
-                w_grouped = stage.tile([P, PACK, P, PACK], BF16, align_bytes=64)
-                src = w_raw[h, c][:].rearrange("p j (q i) -> p q j i", i=PACK)
-                dst = w_grouped[:].rearrange("p i q j -> p q j i")
-                nc.vector.tensor_copy(
-                    out=dst[:, :VECTOR_COLUMNS], in_=src[:, :VECTOR_COLUMNS]
-                )
-                nc.scalar.copy(out=dst[:, VECTOR_COLUMNS:], in_=src[:, VECTOR_COLUMNS:])
-                nc.vector.quantize_mx(
-                    out=w_codes[:, h, c].rearrange("p i q -> p (i q)").bitcast(FP8X4),
-                    scales=w_scales[:, h, c].rearrange("p i q -> p (i q)"),
-                    in_=w_grouped[:].rearrange("p i q j -> p (i q j)"),
-                )
+        t_psum = {}
 
-            t_psum = psum.tile([P, PACK, N], F32)
-            for i in range(PACK):
-                for c in range(PASSES):
-                    nc.tensor.matmul_mx(
-                        out=t_psum[:, i, :],
-                        lhsT=w_codes[:, h, c, i, :].bitcast(FP8X4),
-                        lhsT_scale=w_scales[:, h, c, i, :],
-                        rhs=e_codes[:, c, :].bitcast(FP8X4),
-                        rhs_scale=e_scales[:, c, :],
-                        start=(c == 0),
-                        stop=(c == PASSES - 1),
-                    )
-
+        def contract_half(h):
             t_grouped = stage.tile([P, N, PACK], BF16, align_bytes=64)
-            nc.scalar.copy(out=t_grouped[:], in_=t_psum[:].rearrange("q i n -> q n i"))
+            nc.scalar.copy(out=t_grouped[:], in_=t_psum[h][:].rearrange("q i n -> q n i"))
             nc.vector.quantize_mx(
                 out=t_codes[:, h, :].bitcast(FP8X4),
                 scales=t_scales[:, h, :],
@@ -111,6 +100,44 @@ def tile_parallelcoattention_s_kernel(tc, embedding, heatm, W_b, out):
                 start=(h == 0),
                 stop=(h == PASSES - 1),
             )
+
+        for (h, g, first, tiles), raw in zip(pieces, w_raw):
+            w_grouped = stage.tile([P, tiles * P, PACK], BF16, align_bytes=64)
+            regroup(nc, w_grouped[:], raw[:])
+            for k in range(tiles):
+                nc.vector.quantize_mx(
+                    out=w_codes[:, h, g, first + k, :].bitcast(FP8X4),
+                    scales=w_scales[:, h, g, first + k, :],
+                    in_=w_grouped[:, k * P : (k + 1) * P, :].rearrange("p w t -> p (w t)"),
+                )
+            if h == 0 and g == 0 and first + tiles == PACK:
+                for gg in range(PASSES):
+                    regroup(nc, e_grouped[:, gg], e_raw[:, gg])
+                nc.vector.quantize_mx(
+                    out=e_codes[:].rearrange("p g n -> p (g n)").bitcast(FP8X4),
+                    scales=e_scales[:].rearrange("p g n -> p (g n)"),
+                    in_=e_grouped[:].rearrange("p g n t -> p (g n t)"),
+                )
+            if g < PASSES - 1:
+                if h > 0 and first + tiles == PACK:
+                    contract_half(h - 1)
+                continue
+
+            if first == 0:
+                t_psum[h] = psum.tile([P, PACK, N], F32, name="t_psum")
+            for i in range(first, first + tiles):
+                for gg in range(PASSES):
+                    nc.tensor.matmul_mx(
+                        out=t_psum[h][:, i, :],
+                        lhsT=w_codes[:, h, gg, i, :].bitcast(FP8X4),
+                        lhsT_scale=w_scales[:, h, gg, i, :],
+                        rhs=e_codes[:, gg, :].bitcast(FP8X4),
+                        rhs_scale=e_scales[:, gg, :],
+                        start=(gg == 0),
+                        stop=(gg == PASSES - 1),
+                    )
+
+        contract_half(PASSES - 1)
 
         row_max = keep.tile([P, 1], F32)
         nc.vector.tensor_reduce(out=row_max[:], in_=c_psum[:], axis=AXIS.X, op=ALU.max)

@@ -18,53 +18,30 @@ K_PASS = P * PACK
 D = 1024
 N = 128
 PASSES = D // K_PASS
-RUN = 4
 
-END_PIECES = 2
-
-VECTOR_SIXTEENTHS = 9
+VECTOR_COLUMNS = 76
 
 FLOPS = 2 * N * D * D + 2 * N * N * D
 BYTES = 2 * D * N + 2 * D * D + 4 * N
 
 
-def regroup(nc, grouped, raw):
-    src = raw.rearrange("p t (c i) -> p c t i", i=RUN)
-    dst = grouped.rearrange("p (c i) t -> p c t i", i=RUN)
-    split = src.shape[1] * VECTOR_SIXTEENTHS // 16
-    nc.vector.tensor_copy(out=dst[:, :split], in_=src[:, :split])
-    nc.scalar.copy(out=dst[:, split:], in_=src[:, split:])
-
-
 def tile_parallelcoattention_s_kernel(tc, embedding, heatm, W_b, out):
     nc = tc.nc
-
-    pieces = []
-    for h in range(PASSES):
-        for g in range(PASSES):
-            at_an_end = h == g and h in (0, PASSES - 1)
-            tiles = PACK // END_PIECES if at_an_end else PACK
-            for first in range(0, PACK, tiles):
-                pieces.append((h, g, first, tiles))
-
     with ExitStack() as ctx:
         keep = ctx.enter_context(tc.tile_pool(name="keep", bufs=1))
-        stage = ctx.enter_context(tc.tile_pool(name="stage", bufs=len(pieces)))
+        stage = ctx.enter_context(tc.tile_pool(name="stage", bufs=PASSES * PASSES))
         psum = ctx.enter_context(tc.psum_pool(name="psum", bufs=2))
 
         e_raw = keep.tile([P, PASSES, PACK, N], BF16)
-        w_rows = W_b.rearrange("(g t p) w -> g p t w", t=PACK, p=P)
+        nc.sync.dma_start(
+            out=e_raw[:], in_=embedding[0].rearrange("(c p j) n -> p c j n", p=P, j=PACK)
+        )
+        w_rows = W_b.rearrange("(c p j) w -> c p j w", p=P, j=PACK)
         w_raw = []
-        for h, g, first, tiles in pieces:
-            raw = stage.tile([P, PACK, tiles * P], BF16, name="w_raw")
-            start = h * K_PASS + first * P
-            nc.sync.dma_start(out=raw[:], in_=w_rows[g][:, :, start : start + tiles * P])
+        for c in range(PASSES):
+            raw = keep.tile([P, PACK, D], BF16, name="w_raw%d" % c)
+            nc.sync.dma_start(out=raw[:], in_=w_rows[c])
             w_raw.append(raw)
-            if h == 0 and g == 0 and first + tiles == PACK:
-                nc.sync.dma_start(
-                    out=e_raw[:],
-                    in_=embedding[0].rearrange("(g t p) n -> p g t n", t=PACK, p=P),
-                )
 
         zero = keep.tile([P, 1], F32)
         nc.vector.memset(zero[:], 0.0)
@@ -73,19 +50,54 @@ def tile_parallelcoattention_s_kernel(tc, embedding, heatm, W_b, out):
         ident = keep.tile([P, P], F32)
         make_identity(nc, ident[:])
 
+        e_grouped = keep.tile([P, PASSES, N, PACK], BF16, align_bytes=64)
+        nc.vector.tensor_copy(out=e_grouped[:], in_=e_raw[:].rearrange("p c j n -> p c n j"))
+        e_codes = keep.tile([P, PASSES, N], U32, align_bytes=64)
+        e_scales = keep.tile([P, PASSES, N], U8, align_bytes=64)
+        nc.vector.quantize_mx(
+            out=e_codes[:].rearrange("p c n -> p (c n)").bitcast(FP8X4),
+            scales=e_scales[:].rearrange("p c n -> p (c n)"),
+            in_=e_grouped[:].rearrange("p c n j -> p (c n j)"),
+        )
+
         w_codes = keep.tile([P, PASSES, PASSES, PACK, P], U32, align_bytes=64)
         w_scales = keep.tile([P, PASSES, PASSES, PACK, P], U8, align_bytes=64)
         t_codes = keep.tile([P, PASSES, N], U32, align_bytes=64)
         t_scales = keep.tile([P, PASSES, N], U8, align_bytes=64)
-        e_grouped = keep.tile([P, PASSES, N, PACK], BF16, align_bytes=64)
-        e_codes = keep.tile([P, PASSES, N], U32, align_bytes=64)
-        e_scales = keep.tile([P, PASSES, N], U8, align_bytes=64)
         c_psum = psum.tile([P, N], F32)
-        t_psum = {}
+        for c in range(PASSES):
+            for h in range(PASSES):
+                w_grouped = stage.tile([P, PACK, P, PACK], BF16, align_bytes=64)
+                half = w_raw[c][:, :, h * K_PASS : (h + 1) * K_PASS]
+                src = half.rearrange("p j (q i) -> p q j i", i=PACK)
+                dst = w_grouped[:].rearrange("p i q j -> p q j i")
+                nc.vector.tensor_copy(
+                    out=dst[:, :VECTOR_COLUMNS], in_=src[:, :VECTOR_COLUMNS]
+                )
+                nc.scalar.copy(out=dst[:, VECTOR_COLUMNS:], in_=src[:, VECTOR_COLUMNS:])
+                for i in range(PACK):
+                    nc.vector.quantize_mx(
+                        out=w_codes[:, h, c, i, :].bitcast(FP8X4),
+                        scales=w_scales[:, h, c, i, :],
+                        in_=w_grouped[:, i].rearrange("p q j -> p (q j)"),
+                    )
 
-        def contract_half(h):
+        for h in range(PASSES):
+            t_psum = psum.tile([P, PACK, N], F32)
+            for i in range(PACK):
+                for c in range(PASSES):
+                    nc.tensor.matmul_mx(
+                        out=t_psum[:, i, :],
+                        lhsT=w_codes[:, h, c, i, :].bitcast(FP8X4),
+                        lhsT_scale=w_scales[:, h, c, i, :],
+                        rhs=e_codes[:, c, :].bitcast(FP8X4),
+                        rhs_scale=e_scales[:, c, :],
+                        start=(c == 0),
+                        stop=(c == PASSES - 1),
+                    )
+
             t_grouped = stage.tile([P, N, PACK], BF16, align_bytes=64)
-            nc.scalar.copy(out=t_grouped[:], in_=t_psum[h][:].rearrange("q i n -> q n i"))
+            nc.scalar.copy(out=t_grouped[:], in_=t_psum[:].rearrange("q i n -> q n i"))
             nc.vector.quantize_mx(
                 out=t_codes[:, h, :].bitcast(FP8X4),
                 scales=t_scales[:, h, :],
@@ -100,44 +112,6 @@ def tile_parallelcoattention_s_kernel(tc, embedding, heatm, W_b, out):
                 start=(h == 0),
                 stop=(h == PASSES - 1),
             )
-
-        for (h, g, first, tiles), raw in zip(pieces, w_raw):
-            w_grouped = stage.tile([P, tiles * P, PACK], BF16, align_bytes=64)
-            regroup(nc, w_grouped[:], raw[:])
-            for k in range(tiles):
-                nc.vector.quantize_mx(
-                    out=w_codes[:, h, g, first + k, :].bitcast(FP8X4),
-                    scales=w_scales[:, h, g, first + k, :],
-                    in_=w_grouped[:, k * P : (k + 1) * P, :].rearrange("p w t -> p (w t)"),
-                )
-            if h == 0 and g == 0 and first + tiles == PACK:
-                for gg in range(PASSES):
-                    regroup(nc, e_grouped[:, gg], e_raw[:, gg])
-                nc.vector.quantize_mx(
-                    out=e_codes[:].rearrange("p g n -> p (g n)").bitcast(FP8X4),
-                    scales=e_scales[:].rearrange("p g n -> p (g n)"),
-                    in_=e_grouped[:].rearrange("p g n t -> p (g n t)"),
-                )
-            if g < PASSES - 1:
-                if h > 0 and first + tiles == PACK:
-                    contract_half(h - 1)
-                continue
-
-            if first == 0:
-                t_psum[h] = psum.tile([P, PACK, N], F32, name="t_psum")
-            for i in range(first, first + tiles):
-                for gg in range(PASSES):
-                    nc.tensor.matmul_mx(
-                        out=t_psum[h][:, i, :],
-                        lhsT=w_codes[:, h, gg, i, :].bitcast(FP8X4),
-                        lhsT_scale=w_scales[:, h, gg, i, :],
-                        rhs=e_codes[:, gg, :].bitcast(FP8X4),
-                        rhs_scale=e_scales[:, gg, :],
-                        start=(gg == 0),
-                        stop=(gg == PASSES - 1),
-                    )
-
-        contract_half(PASSES - 1)
 
         row_max = keep.tile([P, 1], F32)
         nc.vector.tensor_reduce(out=row_max[:], in_=c_psum[:], axis=AXIS.X, op=ALU.max)

@@ -19,7 +19,7 @@ D = 1024
 N = 128
 PASSES = D // K_PASS
 
-VECTOR_COLUMNS = 76
+VECTOR_COLUMNS = (72, 72, 56, 64)
 
 FLOPS = 2 * N * D * D + 2 * N * N * D
 BYTES = 2 * D * N + 2 * D * D + 4 * N
@@ -29,8 +29,8 @@ def tile_parallelcoattention_s_kernel(tc, embedding, heatm, W_b, out):
     nc = tc.nc
     with ExitStack() as ctx:
         keep = ctx.enter_context(tc.tile_pool(name="keep", bufs=1))
-        stage = ctx.enter_context(tc.tile_pool(name="stage", bufs=PASSES * PASSES))
         psum = ctx.enter_context(tc.psum_pool(name="psum", bufs=2))
+        ctx.enter_context(tc.manual_schedule(engines={mybir.EngineType.PE}))
 
         e_raw = keep.tile([P, PASSES, PACK, N], BF16)
         nc.sync.dma_start(
@@ -65,29 +65,63 @@ def tile_parallelcoattention_s_kernel(tc, embedding, heatm, W_b, out):
         t_codes = keep.tile([P, PASSES, N], U32, align_bytes=64)
         t_scales = keep.tile([P, PASSES, N], U8, align_bytes=64)
         c_psum = psum.tile([P, N], F32)
-        for c in range(PASSES):
-            for h in range(PASSES):
-                w_grouped = stage.tile([P, PACK, P, PACK], BF16, align_bytes=64)
-                half = w_raw[c][:, :, h * K_PASS : (h + 1) * K_PASS]
-                src = half.rearrange("p j (q i) -> p q j i", i=PACK)
-                dst = w_grouped[:].rearrange("p i q j -> p q j i")
-                nc.vector.tensor_copy(
-                    out=dst[:, :VECTOR_COLUMNS], in_=src[:, :VECTOR_COLUMNS]
-                )
-                nc.scalar.copy(out=dst[:, VECTOR_COLUMNS:], in_=src[:, VECTOR_COLUMNS:])
-                for i in range(PACK):
-                    nc.vector.quantize_mx(
-                        out=w_codes[:, h, c, i, :].bitcast(FP8X4),
-                        scales=w_scales[:, h, c, i, :],
-                        in_=w_grouped[:, i].rearrange("p q j -> p (q j)"),
-                    )
+        w_grouped = {}
 
-        for h in range(PASSES):
-            t_psum = psum.tile([P, PACK, N], F32)
+        def regroup(c, h, vector_columns):
+            grouped = keep.tile([P, PACK, P, PACK], BF16, align_bytes=64, name="w_grouped%d%d" % (c, h))
+            half = w_raw[c][:, :, h * K_PASS : (h + 1) * K_PASS]
+            src = half.rearrange("p j (q i) -> p q j i", i=PACK)
+            dst = grouped[:].rearrange("p i q j -> p q j i")
+            nc.vector.tensor_copy(out=dst[:, :vector_columns], in_=src[:, :vector_columns])
+            nc.scalar.copy(out=dst[:, vector_columns:], in_=src[:, vector_columns:])
+            w_grouped[(c, h)] = grouped
+
+        def quantise_wide(c, h):
+            nc.vector.quantize_mx(
+                out=w_codes[:, h, c].rearrange("p i q -> p (i q)").bitcast(FP8X4),
+                scales=w_scales[:, h, c].rearrange("p i q -> p (i q)"),
+                in_=w_grouped[(c, h)][:].rearrange("p i q j -> p (i q j)"),
+            )
+
+        scratch = psum.tile([P, K_PASS], F32)
+
+        def idle_passes_on_embedding(count):
+            for k in range(count):
+                nc.tensor.matmul_mx(
+                    out=scratch[:, : PASSES * N],
+                    lhsT=e_codes[:, 0, :].bitcast(FP8X4),
+                    lhsT_scale=e_scales[:, 0, :],
+                    rhs=e_codes[:].rearrange("p c n -> p (c n)").bitcast(FP8X4),
+                    rhs_scale=e_scales[:].rearrange("p c n -> p (c n)"),
+                    start=True,
+                    stop=True,
+                )
+
+        def idle_passes_on_w(count, c, h):
+            for k in range(count):
+                nc.tensor.matmul_mx(
+                    out=scratch[:],
+                    lhsT=e_codes[:, c, :].bitcast(FP8X4),
+                    lhsT_scale=e_scales[:, c, :],
+                    rhs=w_codes[:, h, c].rearrange("p i q -> p (i q)").bitcast(FP8X4),
+                    rhs_scale=w_scales[:, h, c].rearrange("p i q -> p (i q)"),
+                    start=True,
+                    stop=True,
+                )
+
+        t_psum = {}
+
+        def first_matmul(h):
+            t_psum[h] = psum.tile([P, PACK, N], F32, name="t_psum")
             for i in range(PACK):
+                nc.vector.quantize_mx(
+                    out=w_codes[:, h, 1, i, :].bitcast(FP8X4),
+                    scales=w_scales[:, h, 1, i, :],
+                    in_=w_grouped[(1, h)][:, i].rearrange("p q j -> p (q j)"),
+                )
                 for c in range(PASSES):
                     nc.tensor.matmul_mx(
-                        out=t_psum[:, i, :],
+                        out=t_psum[h][:, i, :],
                         lhsT=w_codes[:, h, c, i, :].bitcast(FP8X4),
                         lhsT_scale=w_scales[:, h, c, i, :],
                         rhs=e_codes[:, c, :].bitcast(FP8X4),
@@ -96,8 +130,9 @@ def tile_parallelcoattention_s_kernel(tc, embedding, heatm, W_b, out):
                         stop=(c == PASSES - 1),
                     )
 
-            t_grouped = stage.tile([P, N, PACK], BF16, align_bytes=64)
-            nc.scalar.copy(out=t_grouped[:], in_=t_psum[:].rearrange("q i n -> q n i"))
+        def second_matmul(h):
+            t_grouped = keep.tile([P, N, PACK], BF16, align_bytes=64, name="t_grouped%d" % h)
+            nc.scalar.copy(out=t_grouped[:], in_=t_psum[h][:].rearrange("q i n -> q n i"))
             nc.vector.quantize_mx(
                 out=t_codes[:, h, :].bitcast(FP8X4),
                 scales=t_scales[:, h, :],
@@ -112,6 +147,22 @@ def tile_parallelcoattention_s_kernel(tc, embedding, heatm, W_b, out):
                 start=(h == 0),
                 stop=(h == PASSES - 1),
             )
+
+        idle_passes_on_embedding(12)
+        regroup(0, 0, VECTOR_COLUMNS[0])
+        regroup(0, 1, VECTOR_COLUMNS[1])
+        quantise_wide(0, 0)
+        idle_passes_on_w(3, 0, 0)
+        quantise_wide(0, 1)
+        idle_passes_on_w(2, 0, 1)
+        regroup(1, 0, VECTOR_COLUMNS[2])
+        regroup(1, 1, VECTOR_COLUMNS[3])
+        first_matmul(0)
+        first_matmul(1)
+        second_matmul(0)
+        idle_passes_on_w(2, 0, 0)
+        second_matmul(1)
+        idle_passes_on_w(2, 0, 0)
 
         row_max = keep.tile([P, 1], F32)
         nc.vector.tensor_reduce(out=row_max[:], in_=c_psum[:], axis=AXIS.X, op=ALU.max)

@@ -19,7 +19,8 @@ D = 1024
 N = 128
 PASSES = D // K_PASS
 
-VECTOR_COLUMNS = (72, 72, 56, 64)
+VECTOR_COLUMNS = (72, 72, 68, 72)
+PAIR_VECTOR_COLUMNS = 84
 
 FLOPS = 2 * N * D * D + 2 * N * N * D
 BYTES = 2 * D * N + 2 * D * D + 4 * N
@@ -37,11 +38,13 @@ def tile_parallelcoattention_s_kernel(tc, embedding, heatm, W_b, out):
             out=e_raw[:], in_=embedding[0].rearrange("(c p j) n -> p c j n", p=P, j=PACK)
         )
         w_rows = W_b.rearrange("(c p j) w -> c p j w", p=P, j=PACK)
-        w_raw = []
-        for c in range(PASSES):
-            raw = keep.tile([P, PACK, D], BF16, name="w_raw%d" % c)
-            nc.sync.dma_start(out=raw[:], in_=w_rows[c])
-            w_raw.append(raw)
+        w_pair = []
+        for u in range(2):
+            raw = keep.tile([P, 2, D], BF16, name="w_pair%d" % u)
+            nc.sync.dma_start(out=raw[:], in_=w_rows[0][:, 2 * u : 2 * u + 2, :])
+            w_pair.append(raw)
+        w_raw1 = keep.tile([P, PACK, D], BF16)
+        nc.sync.dma_start(out=w_raw1[:], in_=w_rows[1])
 
         zero = keep.tile([P, 1], F32)
         nc.vector.memset(zero[:], 0.0)
@@ -69,12 +72,21 @@ def tile_parallelcoattention_s_kernel(tc, embedding, heatm, W_b, out):
 
         def regroup(c, h, vector_columns):
             grouped = keep.tile([P, PACK, P, PACK], BF16, align_bytes=64, name="w_grouped%d%d" % (c, h))
-            half = w_raw[c][:, :, h * K_PASS : (h + 1) * K_PASS]
+            half = w_raw1[:, :, h * K_PASS : (h + 1) * K_PASS]
             src = half.rearrange("p j (q i) -> p q j i", i=PACK)
             dst = grouped[:].rearrange("p i q j -> p q j i")
             nc.vector.tensor_copy(out=dst[:, :vector_columns], in_=src[:, :vector_columns])
             nc.scalar.copy(out=dst[:, vector_columns:], in_=src[:, vector_columns:])
             w_grouped[(c, h)] = grouped
+
+        def regroup_pair(u, h):
+            if u == 0:
+                w_grouped[(0, h)] = keep.tile([P, PACK, P, PACK], BF16, align_bytes=64, name="w_grouped0%d" % h)
+            half = w_pair[u][:, :, h * K_PASS : (h + 1) * K_PASS]
+            src = half.rearrange("p j (q i) -> p q j i", i=PACK)
+            dst = w_grouped[(0, h)][:].rearrange("p i q j -> p q j i")[:, :, 2 * u : 2 * u + 2, :]
+            nc.vector.tensor_copy(out=dst[:, :PAIR_VECTOR_COLUMNS], in_=src[:, :PAIR_VECTOR_COLUMNS])
+            nc.scalar.copy(out=dst[:, PAIR_VECTOR_COLUMNS:], in_=src[:, PAIR_VECTOR_COLUMNS:])
 
         def quantise_wide(c, h):
             nc.vector.quantize_mx(
@@ -149,8 +161,10 @@ def tile_parallelcoattention_s_kernel(tc, embedding, heatm, W_b, out):
             )
 
         idle_passes_on_embedding(12)
-        regroup(0, 0, VECTOR_COLUMNS[0])
-        regroup(0, 1, VECTOR_COLUMNS[1])
+        regroup_pair(0, 0)
+        regroup_pair(0, 1)
+        regroup_pair(1, 0)
+        regroup_pair(1, 1)
         quantise_wide(0, 0)
         idle_passes_on_w(3, 0, 0)
         quantise_wide(0, 1)

@@ -173,10 +173,11 @@ def tile_parallelcoattention_s_kernel(tc, embedding, heatm, W_b, out):
         regroup(1, 1, VECTOR_COLUMNS[3])
         first_matmul(0)
         first_matmul(1)
+        idle_passes_on_w(2, 0, 0)
         second_matmul(0)
-        idle_passes_on_w(2, 0, 0)
         second_matmul(1)
-        idle_passes_on_w(2, 0, 0)
+        for k in range(3):
+            nc.tensor.transpose(scratch[:, :P], ident[:], ident[:])
 
         row_max = keep.tile([P, 1], F32)
         nc.vector.tensor_reduce(out=row_max[:], in_=c_psum[:], axis=AXIS.X, op=ALU.max)

@@ -30,7 +30,7 @@ def tile_parallelcoattention_s_kernel(tc, embedding, heatm, W_b, out):
     nc = tc.nc
     with ExitStack() as ctx:
         keep = ctx.enter_context(tc.tile_pool(name="keep", bufs=1))
-        psum = ctx.enter_context(tc.psum_pool(name="psum", bufs=2))
+        psum = ctx.enter_context(tc.psum_pool(name="psum", bufs=1))
         ctx.enter_context(tc.manual_schedule(engines={mybir.EngineType.PE}))
 
         e_raw = keep.tile([P, PASSES, PACK, N], BF16)
@@ -124,7 +124,10 @@ def tile_parallelcoattention_s_kernel(tc, embedding, heatm, W_b, out):
         t_psum = {}
 
         def first_matmul(h):
-            t_psum[h] = psum.tile([P, PACK, N], F32, name="t_psum")
+            banks = h + 1
+            t_psum[h] = [
+                psum.tile([P, PACK // banks, N], F32, name="t_psum%d%d" % (h, b)) for b in range(banks)
+            ]
             for i in range(PACK):
                 nc.vector.quantize_mx(
                     out=w_codes[:, h, 1, i, :].bitcast(FP8X4),
@@ -133,7 +136,7 @@ def tile_parallelcoattention_s_kernel(tc, embedding, heatm, W_b, out):
                 )
                 for c in range(PASSES):
                     nc.tensor.matmul_mx(
-                        out=t_psum[h][:, i, :],
+                        out=t_psum[h][i * banks // PACK][:, i % (PACK // banks), :],
                         lhsT=w_codes[:, h, c, i, :].bitcast(FP8X4),
                         lhsT_scale=w_scales[:, h, c, i, :],
                         rhs=e_codes[:, c, :].bitcast(FP8X4),
@@ -142,13 +145,15 @@ def tile_parallelcoattention_s_kernel(tc, embedding, heatm, W_b, out):
                         stop=(c == PASSES - 1),
                     )
 
+        t_grouped = [
+            keep.tile([P, N, PACK], BF16, align_bytes=64, name="t_grouped%d" % h) for h in range(PASSES)
+        ]
+
         def second_matmul(h):
-            t_grouped = keep.tile([P, N, PACK], BF16, align_bytes=64, name="t_grouped%d" % h)
-            nc.scalar.copy(out=t_grouped[:], in_=t_psum[h][:].rearrange("q i n -> q n i"))
             nc.vector.quantize_mx(
                 out=t_codes[:, h, :].bitcast(FP8X4),
                 scales=t_scales[:, h, :],
-                in_=t_grouped[:].rearrange("q n i -> q (n i)"),
+                in_=t_grouped[h][:].rearrange("q n i -> q (n i)"),
             )
             nc.tensor.matmul_mx(
                 out=c_psum[:],
@@ -174,6 +179,9 @@ def tile_parallelcoattention_s_kernel(tc, embedding, heatm, W_b, out):
         first_matmul(0)
         first_matmul(1)
         idle_passes_on_w(2, 0, 0)
+        nc.scalar.copy(out=t_grouped[0][:], in_=t_psum[0][0][:].rearrange("q i n -> q n i"))
+        nc.vector.tensor_copy(out=t_grouped[1][:, :, 0:2], in_=t_psum[1][0][:].rearrange("q i n -> q n i"))
+        nc.scalar.copy(out=t_grouped[1][:, :, 2:4], in_=t_psum[1][1][:].rearrange("q i n -> q n i"))
         second_matmul(0)
         second_matmul(1)
         for k in range(3):

@@ -21,6 +21,7 @@ PASSES = D // K_PASS
 
 VECTOR_COLUMNS = (72, 72, 68, 72)
 PAIR_VECTOR_COLUMNS = 84
+E_VECTOR_COLUMNS = 80
 
 FLOPS = 2 * N * D * D + 2 * N * N * D
 BYTES = 2 * D * N + 2 * D * D + 4 * N
@@ -54,7 +55,9 @@ def tile_parallelcoattention_s_kernel(tc, embedding, heatm, W_b, out):
         make_identity(nc, ident[:])
 
         e_grouped = keep.tile([P, PASSES, N, PACK], BF16, align_bytes=64)
-        nc.vector.tensor_copy(out=e_grouped[:], in_=e_raw[:].rearrange("p c j n -> p c n j"))
+        e_src = e_raw[:].rearrange("p c j n -> p c n j")
+        nc.vector.tensor_copy(out=e_grouped[:, :, :E_VECTOR_COLUMNS], in_=e_src[:, :, :E_VECTOR_COLUMNS])
+        nc.scalar.copy(out=e_grouped[:, :, E_VECTOR_COLUMNS:], in_=e_src[:, :, E_VECTOR_COLUMNS:])
         e_codes = keep.tile([P, PASSES, N], U32, align_bytes=64)
         e_scales = keep.tile([P, PASSES, N], U8, align_bytes=64)
         nc.vector.quantize_mx(

@@ -20,7 +20,9 @@ N = 128
 PASSES = D // K_PASS
 
 VECTOR_COLUMNS = (72, 72, 68, 72)
-PAIR_VECTOR_COLUMNS = 84
+TENSOR_COLUMNS = 56
+PAIR_VECTOR_COLUMNS = (84, 64)
+PAIR_SCALAR_END = (128, 128 - TENSOR_COLUMNS)
 E_VECTOR_COLUMNS = 80
 
 FLOPS = 2 * N * D * D + 2 * N * N * D
@@ -32,7 +34,11 @@ def tile_parallelcoattention_s_kernel(tc, embedding, heatm, W_b, out):
     with ExitStack() as ctx:
         keep = ctx.enter_context(tc.tile_pool(name="keep", bufs=1))
         psum = ctx.enter_context(tc.psum_pool(name="psum", bufs=1))
-        ctx.enter_context(tc.manual_schedule(engines={mybir.EngineType.PE}))
+        ctx.enter_context(
+            tc.manual_schedule(
+                engines={mybir.EngineType.PE, mybir.EngineType.DVE, mybir.EngineType.Activation}
+            )
+        )
 
         e_raw = keep.tile([P, PASSES, PACK, N], BF16)
         nc.sync.dma_start(
@@ -51,6 +57,8 @@ def tile_parallelcoattention_s_kernel(tc, embedding, heatm, W_b, out):
         nc.vector.memset(zero[:], 0.0)
         warm = keep.tile([P, 1], F32)
         nc.scalar.activation(out=warm[:], in_=zero[:], func=ACT.Tanh)
+        ident_bf16 = keep.tile([P, P], BF16)
+        make_identity(nc, ident_bf16[:])
         ident = keep.tile([P, P], F32)
         make_identity(nc, ident[:])
 
@@ -88,8 +96,24 @@ def tile_parallelcoattention_s_kernel(tc, embedding, heatm, W_b, out):
             half = w_pair[u][:, :, h * K_PASS : (h + 1) * K_PASS]
             src = half.rearrange("p j (q i) -> p q j i", i=PACK)
             dst = w_grouped[(0, h)][:].rearrange("p i q j -> p q j i")[:, :, 2 * u : 2 * u + 2, :]
-            nc.vector.tensor_copy(out=dst[:, :PAIR_VECTOR_COLUMNS], in_=src[:, :PAIR_VECTOR_COLUMNS])
-            nc.scalar.copy(out=dst[:, PAIR_VECTOR_COLUMNS:], in_=src[:, PAIR_VECTOR_COLUMNS:])
+            first, last = PAIR_VECTOR_COLUMNS[h], PAIR_SCALAR_END[h]
+            nc.vector.tensor_copy(out=dst[:, :first], in_=src[:, :first])
+            nc.scalar.copy(out=dst[:, first:last], in_=src[:, first:last])
+
+        w_interleaved = psum.tile([P, TENSOR_COLUMNS * PACK, PACK], BF16)
+
+        def interleave_pair(u):
+            nc.tensor.matmul(
+                out=w_interleaved[:, :, 2 * u : 2 * u + 2],
+                lhsT=ident_bf16[:],
+                rhs=w_pair[u][:, :, D - TENSOR_COLUMNS * PACK :].rearrange("p j c -> p c j"),
+                start=True,
+                stop=True,
+            )
+
+        def copy_interleaved():
+            src = w_interleaved[:].rearrange("p (q i) j -> p i q j", i=PACK)
+            nc.scalar.copy(out=w_grouped[(0, 1)][:, :, PAIR_SCALAR_END[1] :, :], in_=src)
 
         def quantise_wide(c, h):
             nc.vector.quantize_mx(
@@ -168,11 +192,15 @@ def tile_parallelcoattention_s_kernel(tc, embedding, heatm, W_b, out):
                 stop=(h == PASSES - 1),
             )
 
-        idle_passes_on_embedding(12)
+        interleave_pair(0)
+        idle_passes_on_embedding(3)
+        interleave_pair(1)
+        idle_passes_on_embedding(6)
         regroup_pair(0, 0)
         regroup_pair(0, 1)
         regroup_pair(1, 0)
         regroup_pair(1, 1)
+        copy_interleaved()
         quantise_wide(0, 0)
         idle_passes_on_w(3, 0, 0)
         quantise_wide(0, 1)

@@ -19,10 +19,10 @@ D = 1024
 N = 128
 PASSES = D // K_PASS
 
-VECTOR_COLUMNS = (72, 72, 68, 72)
+VECTOR_COLUMNS = (68, 50)
 TENSOR_COLUMNS = 56
-PAIR_VECTOR_COLUMNS = (84, 64)
-PAIR_SCALAR_END = (128, 128 - TENSOR_COLUMNS)
+SCALAR_END = (128, 128 - TENSOR_COLUMNS)
+PAIR_VECTOR_COLUMNS = 84
 E_VECTOR_COLUMNS = 80
 
 FLOPS = 2 * N * D * D + 2 * N * N * D
@@ -81,14 +81,15 @@ def tile_parallelcoattention_s_kernel(tc, embedding, heatm, W_b, out):
         c_psum = psum.tile([P, N], F32)
         w_grouped = {}
 
-        def regroup(c, h, vector_columns):
-            grouped = keep.tile([P, PACK, P, PACK], BF16, align_bytes=64, name="w_grouped%d%d" % (c, h))
+        def regroup(h):
+            grouped = keep.tile([P, PACK, P, PACK], BF16, align_bytes=64, name="w_grouped1%d" % h)
             half = w_raw1[:, :, h * K_PASS : (h + 1) * K_PASS]
             src = half.rearrange("p j (q i) -> p q j i", i=PACK)
             dst = grouped[:].rearrange("p i q j -> p q j i")
-            nc.vector.tensor_copy(out=dst[:, :vector_columns], in_=src[:, :vector_columns])
-            nc.scalar.copy(out=dst[:, vector_columns:], in_=src[:, vector_columns:])
-            w_grouped[(c, h)] = grouped
+            first, last = VECTOR_COLUMNS[h], SCALAR_END[h]
+            nc.vector.tensor_copy(out=dst[:, :first], in_=src[:, :first])
+            nc.scalar.copy(out=dst[:, first:last], in_=src[:, first:last])
+            w_grouped[(1, h)] = grouped
 
         def regroup_pair(u, h):
             if u == 0:
@@ -96,9 +97,8 @@ def tile_parallelcoattention_s_kernel(tc, embedding, heatm, W_b, out):
             half = w_pair[u][:, :, h * K_PASS : (h + 1) * K_PASS]
             src = half.rearrange("p j (q i) -> p q j i", i=PACK)
             dst = w_grouped[(0, h)][:].rearrange("p i q j -> p q j i")[:, :, 2 * u : 2 * u + 2, :]
-            first, last = PAIR_VECTOR_COLUMNS[h], PAIR_SCALAR_END[h]
-            nc.vector.tensor_copy(out=dst[:, :first], in_=src[:, :first])
-            nc.scalar.copy(out=dst[:, first:last], in_=src[:, first:last])
+            nc.vector.tensor_copy(out=dst[:, :PAIR_VECTOR_COLUMNS], in_=src[:, :PAIR_VECTOR_COLUMNS])
+            nc.scalar.copy(out=dst[:, PAIR_VECTOR_COLUMNS:], in_=src[:, PAIR_VECTOR_COLUMNS:])
 
         w_interleaved = psum.tile([P, TENSOR_COLUMNS * PACK, PACK], BF16)
 
@@ -106,14 +106,14 @@ def tile_parallelcoattention_s_kernel(tc, embedding, heatm, W_b, out):
             nc.tensor.matmul(
                 out=w_interleaved[:, :, 2 * u : 2 * u + 2],
                 lhsT=ident_bf16[:],
-                rhs=w_pair[u][:, :, D - TENSOR_COLUMNS * PACK :].rearrange("p j c -> p c j"),
+                rhs=w_raw1[:, 2 * u : 2 * u + 2, D - TENSOR_COLUMNS * PACK :].rearrange("p j c -> p c j"),
                 start=True,
                 stop=True,
             )
 
-        def copy_interleaved():
+        def copy_interleaved(tiles):
             src = w_interleaved[:].rearrange("p (q i) j -> p i q j", i=PACK)
-            nc.scalar.copy(out=w_grouped[(0, 1)][:, :, PAIR_SCALAR_END[1] :, :], in_=src)
+            nc.scalar.copy(out=w_grouped[(1, 1)][:, tiles, SCALAR_END[1] :, :], in_=src[:, tiles])
 
         def quantise_wide(c, h):
             nc.vector.quantize_mx(
@@ -192,21 +192,21 @@ def tile_parallelcoattention_s_kernel(tc, embedding, heatm, W_b, out):
                 stop=(h == PASSES - 1),
             )
 
-        interleave_pair(0)
-        idle_passes_on_embedding(3)
-        interleave_pair(1)
-        idle_passes_on_embedding(6)
+        idle_passes_on_embedding(12)
         regroup_pair(0, 0)
         regroup_pair(0, 1)
         regroup_pair(1, 0)
         regroup_pair(1, 1)
-        copy_interleaved()
         quantise_wide(0, 0)
         idle_passes_on_w(3, 0, 0)
         quantise_wide(0, 1)
+        interleave_pair(0)
+        interleave_pair(1)
         idle_passes_on_w(2, 0, 1)
-        regroup(1, 0, VECTOR_COLUMNS[2])
-        regroup(1, 1, VECTOR_COLUMNS[3])
+        regroup(0)
+        regroup(1)
+        copy_interleaved(slice(0, 2))
+        copy_interleaved(slice(2, 4))
         first_matmul(0)
         first_matmul(1)
         idle_passes_on_w(2, 0, 0)

@@ -19,7 +19,7 @@ D = 1024
 N = 128
 PASSES = D // K_PASS
 
-VECTOR_COLUMNS = (68, 50)
+VECTOR_COLUMNS = (68, 58)
 TENSOR_COLUMNS = 56
 SCALAR_END = (128, 128 - TENSOR_COLUMNS)
 PAIR_VECTOR_COLUMNS = 84
@@ -100,20 +100,21 @@ def tile_parallelcoattention_s_kernel(tc, embedding, heatm, W_b, out):
             nc.vector.tensor_copy(out=dst[:, :PAIR_VECTOR_COLUMNS], in_=src[:, :PAIR_VECTOR_COLUMNS])
             nc.scalar.copy(out=dst[:, PAIR_VECTOR_COLUMNS:], in_=src[:, PAIR_VECTOR_COLUMNS:])
 
-        w_interleaved = psum.tile([P, TENSOR_COLUMNS * PACK, PACK], BF16)
+        w_interleaved = psum.tile([P, PACK, TENSOR_COLUMNS, PACK], BF16)
 
         def interleave_pair(u):
             nc.tensor.matmul(
-                out=w_interleaved[:, :, 2 * u : 2 * u + 2],
+                out=w_interleaved[:, :, :, 2 * u : 2 * u + 2].rearrange("p i q j -> p j q i"),
                 lhsT=ident_bf16[:],
-                rhs=w_raw1[:, 2 * u : 2 * u + 2, D - TENSOR_COLUMNS * PACK :].rearrange("p j c -> p c j"),
+                rhs=w_raw1[:, 2 * u : 2 * u + 2, D - TENSOR_COLUMNS * PACK :].rearrange(
+                    "p j (q i) -> p j q i", i=PACK
+                ),
                 start=True,
                 stop=True,
             )
 
         def copy_interleaved(tiles):
-            src = w_interleaved[:].rearrange("p (q i) j -> p i q j", i=PACK)
-            nc.scalar.copy(out=w_grouped[(1, 1)][:, tiles, SCALAR_END[1] :, :], in_=src[:, tiles])
+            nc.scalar.copy(out=w_grouped[(1, 1)][:, tiles, SCALAR_END[1] :, :], in_=w_interleaved[:, tiles])
 
         def quantise_wide(c, h):
             nc.vector.quantize_mx(
@@ -192,17 +193,16 @@ def tile_parallelcoattention_s_kernel(tc, embedding, heatm, W_b, out):
                 stop=(h == PASSES - 1),
             )
 
-        idle_passes_on_embedding(12)
+        idle_passes_on_embedding(16)
         regroup_pair(0, 0)
         regroup_pair(0, 1)
         regroup_pair(1, 0)
         regroup_pair(1, 1)
         quantise_wide(0, 0)
-        idle_passes_on_w(3, 0, 0)
         quantise_wide(0, 1)
         interleave_pair(0)
         interleave_pair(1)
-        idle_passes_on_w(2, 0, 1)
+        idle_passes_on_w(2, 0, 0)
         regroup(0)
         regroup(1)
         copy_interleaved(slice(0, 2))

@@ -236,7 +236,11 @@ def tile_parallelcoattention_s_kernel(tc, embedding, heatm, W_b, out):
         )
         inverse = keep.tile([P, 1], F32)
         nc.vector.reciprocal(out=inverse[:], in_=total[:])
-        weights = keep.tile([P, N], F32)
-        nc.vector.tensor_scalar_mul(out=weights[:], in0=e[:], scalar1=inverse[:])
+        weights = keep.tile([P, 2, N], F32)
+        nc.vector.tensor_scalar_mul(
+            out=weights[:, :, : N // 2], in0=e[:].rearrange("p (a n) -> p a n", a=2), scalar1=inverse[:]
+        )
 
-        nc.sync.dma_start(out=out.rearrange("b n o -> b (n o)"), in_=weights[0:1, :])
+        nc.sync.dma_start(
+            out=out.rearrange("b (a n) o -> b a (n o)", a=2), in_=weights[0:1, :, : N // 2]
+        )

@@ -19,7 +19,7 @@ D = 1024
 N = 128
 PASSES = D // K_PASS
 
-VECTOR_COLUMNS = (68, 58)
+VECTOR_COLUMNS = (66, 56)
 TENSOR_COLUMNS = 56
 SCALAR_END = (128, 128 - TENSOR_COLUMNS)
 PAIR_VECTOR_COLUMNS = 84
@@ -45,11 +45,11 @@ def tile_parallelcoattention_s_kernel(tc, embedding, heatm, W_b, out):
             out=e_raw[:], in_=embedding[0].rearrange("(c p j) n -> p c j n", p=P, j=PACK)
         )
         w_rows = W_b.rearrange("(c p j) w -> c p j w", p=P, j=PACK)
-        w_pair = []
+        w_raw0 = keep.tile([P, PACK, D], BF16)
         for u in range(2):
-            raw = keep.tile([P, 2, D], BF16, name="w_pair%d" % u)
-            nc.sync.dma_start(out=raw[:], in_=w_rows[0][:, 2 * u : 2 * u + 2, :])
-            w_pair.append(raw)
+            nc.sync.dma_start(
+                out=w_raw0[:, 2 * u : 2 * u + 2, :], in_=w_rows[0][:, 2 * u : 2 * u + 2, :]
+            )
         w_raw1 = keep.tile([P, PACK, D], BF16)
         nc.sync.dma_start(out=w_raw1[:], in_=w_rows[1])
 
@@ -81,6 +81,11 @@ def tile_parallelcoattention_s_kernel(tc, embedding, heatm, W_b, out):
         c_psum = psum.tile([P, N], F32)
         w_grouped = {}
 
+        def scalar_copy(dst, src):
+            nc.scalar.copy(
+                out=dst.rearrange("p (q r) j i -> p q j r i", r=2), in_=src.rearrange("p (q r) j i -> p q j r i", r=2)
+            )
+
         def regroup(h):
             grouped = keep.tile([P, PACK, P, PACK], BF16, align_bytes=64, name="w_grouped1%d" % h)
             half = w_raw1[:, :, h * K_PASS : (h + 1) * K_PASS]
@@ -88,17 +93,26 @@ def tile_parallelcoattention_s_kernel(tc, embedding, heatm, W_b, out):
             dst = grouped[:].rearrange("p i q j -> p q j i")
             first, last = VECTOR_COLUMNS[h], SCALAR_END[h]
             nc.vector.tensor_copy(out=dst[:, :first], in_=src[:, :first])
-            nc.scalar.copy(out=dst[:, first:last], in_=src[:, first:last])
+            scalar_copy(dst[:, first:last], src[:, first:last])
             w_grouped[(1, h)] = grouped
 
+        for h in range(PASSES):
+            w_grouped[(0, h)] = keep.tile([P, PACK, P, PACK], BF16, align_bytes=64, name="w_grouped0%d" % h)
+
+        def pass0_views(h):
+            half = w_raw0[:, :, h * K_PASS : (h + 1) * K_PASS]
+            return half.rearrange("p j (q i) -> p q j i", i=PACK), w_grouped[(0, h)][:].rearrange("p i q j -> p q j i")
+
         def regroup_pair(u, h):
-            if u == 0:
-                w_grouped[(0, h)] = keep.tile([P, PACK, P, PACK], BF16, align_bytes=64, name="w_grouped0%d" % h)
-            half = w_pair[u][:, :, h * K_PASS : (h + 1) * K_PASS]
-            src = half.rearrange("p j (q i) -> p q j i", i=PACK)
-            dst = w_grouped[(0, h)][:].rearrange("p i q j -> p q j i")[:, :, 2 * u : 2 * u + 2, :]
-            nc.vector.tensor_copy(out=dst[:, :PAIR_VECTOR_COLUMNS], in_=src[:, :PAIR_VECTOR_COLUMNS])
-            nc.scalar.copy(out=dst[:, PAIR_VECTOR_COLUMNS:], in_=src[:, PAIR_VECTOR_COLUMNS:])
+            src, dst = pass0_views(h)
+            rows = slice(2 * u, 2 * u + 2)
+            nc.vector.tensor_copy(
+                out=dst[:, :PAIR_VECTOR_COLUMNS, rows], in_=src[:, :PAIR_VECTOR_COLUMNS, rows]
+            )
+
+        def regroup_whole(h):
+            src, dst = pass0_views(h)
+            scalar_copy(dst[:, PAIR_VECTOR_COLUMNS:], src[:, PAIR_VECTOR_COLUMNS:])
 
         w_interleaved = psum.tile([P, PACK, TENSOR_COLUMNS, PACK], BF16)
 
@@ -198,6 +212,8 @@ def tile_parallelcoattention_s_kernel(tc, embedding, heatm, W_b, out):
         regroup_pair(0, 1)
         regroup_pair(1, 0)
         regroup_pair(1, 1)
+        regroup_whole(0)
+        regroup_whole(1)
         quantise_wide(0, 0)
         quantise_wide(0, 1)
         interleave_pair(0)

@@ -19,7 +19,7 @@ D = 1024
 N = 128
 PASSES = D // K_PASS
 
-VECTOR_COLUMNS = (66, 56)
+VECTOR_COLUMNS = (62, 52)
 TENSOR_COLUMNS = 56
 SCALAR_END = (128, 128 - TENSOR_COLUMNS)
 PAIR_VECTOR_COLUMNS = 84

from contextlib import ExitStack

import concourse.mybir as mybir
from concourse.masks import make_identity

BF16 = mybir.dt.bfloat16
F32 = mybir.dt.float32
U32 = mybir.dt.uint32
U8 = mybir.dt.uint8
FP8X4 = mybir.dt.float8_e4m3fn_x4
ACT = mybir.ActivationFunctionType
ALU = mybir.AluOpType
AXIS = mybir.AxisListType

P = 128
PACK = 4
K_PASS = P * PACK
D = 1024
N = 128
PASSES = D // K_PASS

VECTOR_COLUMNS = (62, 52)
TENSOR_COLUMNS = 56
SCALAR_END = (128, 128 - TENSOR_COLUMNS)
PAIR_VECTOR_COLUMNS = 84
E_VECTOR_COLUMNS = 80

FLOPS = 2 * N * D * D + 2 * N * N * D
BYTES = 2 * D * N + 2 * D * D + 4 * N


def tile_parallelcoattention_s_kernel(tc, embedding, heatm, W_b, out):
    nc = tc.nc
    with ExitStack() as ctx:
        keep = ctx.enter_context(tc.tile_pool(name="keep", bufs=1))
        psum = ctx.enter_context(tc.psum_pool(name="psum", bufs=1))
        ctx.enter_context(
            tc.manual_schedule(
                engines={mybir.EngineType.PE, mybir.EngineType.DVE, mybir.EngineType.Activation}
            )
        )

        e_raw = keep.tile([P, PASSES, PACK, N], BF16)
        nc.sync.dma_start(
            out=e_raw[:], in_=embedding[0].rearrange("(c p j) n -> p c j n", p=P, j=PACK)
        )
        w_rows = W_b.rearrange("(c p j) w -> c p j w", p=P, j=PACK)
        w_raw0 = keep.tile([P, PACK, D], BF16)
        for u in range(2):
            nc.sync.dma_start(
                out=w_raw0[:, 2 * u : 2 * u + 2, :], in_=w_rows[0][:, 2 * u : 2 * u + 2, :]
            )
        w_raw1 = keep.tile([P, PACK, D], BF16)
        nc.sync.dma_start(out=w_raw1[:], in_=w_rows[1])

        zero = keep.tile([P, 1], F32)
        nc.vector.memset(zero[:], 0.0)
        warm = keep.tile([P, 1], F32)
        nc.scalar.activation(out=warm[:], in_=zero[:], func=ACT.Tanh)
        ident_bf16 = keep.tile([P, P], BF16)
        make_identity(nc, ident_bf16[:])
        ident = keep.tile([P, P], F32)
        make_identity(nc, ident[:])

        e_grouped = keep.tile([P, PASSES, N, PACK], BF16, align_bytes=64)
        e_src = e_raw[:].rearrange("p c j n -> p c n j")
        nc.vector.tensor_copy(out=e_grouped[:, :, :E_VECTOR_COLUMNS], in_=e_src[:, :, :E_VECTOR_COLUMNS])
        nc.scalar.copy(out=e_grouped[:, :, E_VECTOR_COLUMNS:], in_=e_src[:, :, E_VECTOR_COLUMNS:])
        e_codes = keep.tile([P, PASSES, N], U32, align_bytes=64)
        e_scales = keep.tile([P, PASSES, N], U8, align_bytes=64)
        nc.vector.quantize_mx(
            out=e_codes[:].rearrange("p c n -> p (c n)").bitcast(FP8X4),
            scales=e_scales[:].rearrange("p c n -> p (c n)"),
            in_=e_grouped[:].rearrange("p c n j -> p (c n j)"),
        )

        w_codes = keep.tile([P, PASSES, PASSES, PACK, P], U32, align_bytes=64)
        w_scales = keep.tile([P, PASSES, PASSES, PACK, P], U8, align_bytes=64)
        t_codes = keep.tile([P, PASSES, N], U32, align_bytes=64)
        t_scales = keep.tile([P, PASSES, N], U8, align_bytes=64)
        c_psum = psum.tile([P, N], F32)
        w_grouped = {}

        def scalar_copy(dst, src):
            nc.scalar.copy(
                out=dst.rearrange("p (q r) j i -> p q j r i", r=2), in_=src.rearrange("p (q r) j i -> p q j r i", r=2)
            )

        def regroup(h):
            grouped = keep.tile([P, PACK, P, PACK], BF16, align_bytes=64, name="w_grouped1%d" % h)
            half = w_raw1[:, :, h * K_PASS : (h + 1) * K_PASS]
            src = half.rearrange("p j (q i) -> p q j i", i=PACK)
            dst = grouped[:].rearrange("p i q j -> p q j i")
            first, last = VECTOR_COLUMNS[h], SCALAR_END[h]
            nc.vector.tensor_copy(out=dst[:, :first], in_=src[:, :first])
            scalar_copy(dst[:, first:last], src[:, first:last])
            w_grouped[(1, h)] = grouped

        for h in range(PASSES):
            w_grouped[(0, h)] = keep.tile([P, PACK, P, PACK], BF16, align_bytes=64, name="w_grouped0%d" % h)

        def pass0_views(h):
            half = w_raw0[:, :, h * K_PASS : (h + 1) * K_PASS]
            return half.rearrange("p j (q i) -> p q j i", i=PACK), w_grouped[(0, h)][:].rearrange("p i q j -> p q j i")

        def regroup_pair(u, h):
            src, dst = pass0_views(h)
            rows = slice(2 * u, 2 * u + 2)
            nc.vector.tensor_copy(
                out=dst[:, :PAIR_VECTOR_COLUMNS, rows], in_=src[:, :PAIR_VECTOR_COLUMNS, rows]
            )

        def regroup_whole(h):
            src, dst = pass0_views(h)
            scalar_copy(dst[:, PAIR_VECTOR_COLUMNS:], src[:, PAIR_VECTOR_COLUMNS:])

        w_interleaved = psum.tile([P, PACK, TENSOR_COLUMNS, PACK], BF16)

        def interleave_pair(u):
            nc.tensor.matmul(
                out=w_interleaved[:, :, :, 2 * u : 2 * u + 2].rearrange("p i q j -> p j q i"),
                lhsT=ident_bf16[:],
                rhs=w_raw1[:, 2 * u : 2 * u + 2, D - TENSOR_COLUMNS * PACK :].rearrange(
                    "p j (q i) -> p j q i", i=PACK
                ),
                start=True,
                stop=True,
            )

        def copy_interleaved(tiles):
            nc.scalar.copy(out=w_grouped[(1, 1)][:, tiles, SCALAR_END[1] :, :], in_=w_interleaved[:, tiles])

        def quantise_wide(c, h):
            nc.vector.quantize_mx(
                out=w_codes[:, h, c].rearrange("p i q -> p (i q)").bitcast(FP8X4),
                scales=w_scales[:, h, c].rearrange("p i q -> p (i q)"),
                in_=w_grouped[(c, h)][:].rearrange("p i q j -> p (i q j)"),
            )

        scratch = psum.tile([P, K_PASS], F32)

        def idle_passes_on_embedding(count):
            for k in range(count):
                nc.tensor.matmul_mx(
                    out=scratch[:, : PASSES * N],
                    lhsT=e_codes[:, 0, :].bitcast(FP8X4),
                    lhsT_scale=e_scales[:, 0, :],
                    rhs=e_codes[:].rearrange("p c n -> p (c n)").bitcast(FP8X4),
                    rhs_scale=e_scales[:].rearrange("p c n -> p (c n)"),
                    start=True,
                    stop=True,
                )

        def idle_passes_on_w(count, c, h):
            for k in range(count):
                nc.tensor.matmul_mx(
                    out=scratch[:],
                    lhsT=e_codes[:, c, :].bitcast(FP8X4),
                    lhsT_scale=e_scales[:, c, :],
                    rhs=w_codes[:, h, c].rearrange("p i q -> p (i q)").bitcast(FP8X4),
                    rhs_scale=w_scales[:, h, c].rearrange("p i q -> p (i q)"),
                    start=True,
                    stop=True,
                )

        t_psum = {}

        def first_matmul(h):
            banks = h + 1
            t_psum[h] = [
                psum.tile([P, PACK // banks, N], F32, name="t_psum%d%d" % (h, b)) for b in range(banks)
            ]
            for i in range(PACK):
                nc.vector.quantize_mx(
                    out=w_codes[:, h, 1, i, :].bitcast(FP8X4),
                    scales=w_scales[:, h, 1, i, :],
                    in_=w_grouped[(1, h)][:, i].rearrange("p q j -> p (q j)"),
                )
                for c in range(PASSES):
                    nc.tensor.matmul_mx(
                        out=t_psum[h][i * banks // PACK][:, i % (PACK // banks), :],
                        lhsT=w_codes[:, h, c, i, :].bitcast(FP8X4),
                        lhsT_scale=w_scales[:, h, c, i, :],
                        rhs=e_codes[:, c, :].bitcast(FP8X4),
                        rhs_scale=e_scales[:, c, :],
                        start=(c == 0),
                        stop=(c == PASSES - 1),
                    )

        t_grouped = [
            keep.tile([P, N, PACK], BF16, align_bytes=64, name="t_grouped%d" % h) for h in range(PASSES)
        ]

        def second_matmul(h):
            nc.vector.quantize_mx(
                out=t_codes[:, h, :].bitcast(FP8X4),
                scales=t_scales[:, h, :],
                in_=t_grouped[h][:].rearrange("q n i -> q (n i)"),
            )
            nc.tensor.matmul_mx(
                out=c_psum[:],
                lhsT=t_codes[:, h, :].bitcast(FP8X4),
                lhsT_scale=t_scales[:, h, :],
                rhs=e_codes[:, h, :].bitcast(FP8X4),
                rhs_scale=e_scales[:, h, :],
                start=(h == 0),
                stop=(h == PASSES - 1),
            )

        idle_passes_on_embedding(16)
        regroup_pair(0, 0)
        regroup_pair(0, 1)
        regroup_pair(1, 0)
        regroup_pair(1, 1)
        regroup_whole(0)
        regroup_whole(1)
        quantise_wide(0, 0)
        quantise_wide(0, 1)
        interleave_pair(0)
        interleave_pair(1)
        idle_passes_on_w(2, 0, 0)
        regroup(0)
        regroup(1)
        copy_interleaved(slice(0, 2))
        copy_interleaved(slice(2, 4))
        first_matmul(0)
        first_matmul(1)
        idle_passes_on_w(2, 0, 0)
        nc.scalar.copy(out=t_grouped[0][:], in_=t_psum[0][0][:].rearrange("q i n -> q n i"))
        nc.vector.tensor_copy(out=t_grouped[1][:, :, 0:2], in_=t_psum[1][0][:].rearrange("q i n -> q n i"))
        nc.scalar.copy(out=t_grouped[1][:, :, 2:4], in_=t_psum[1][1][:].rearrange("q i n -> q n i"))
        second_matmul(0)
        second_matmul(1)
        for k in range(3):
            nc.tensor.transpose(scratch[:, :P], ident[:], ident[:])

        row_max = keep.tile([P, 1], F32)
        nc.vector.tensor_reduce(out=row_max[:], in_=c_psum[:], axis=AXIS.X, op=ALU.max)
        m = keep.tile([P, 1], F32)
        nc.scalar.activation(out=m[:], in_=row_max[:], func=ACT.Tanh)

        m_rows = psum.tile([P, N], F32)
        nc.tensor.transpose(m_rows[:], m[:, 0:1].to_broadcast([P, P]), ident[:])
        minus_top = keep.tile([P, 1], F32)
        nc.vector.tensor_reduce(
            out=minus_top[:], in_=m_rows[:], axis=AXIS.X, op=ALU.max, negate=True
        )
        e = keep.tile([P, N], F32)
        total = keep.tile([P, 1], F32)
        nc.scalar.activation(
            out=e[:], in_=m_rows[:], func=ACT.Exp, bias=minus_top[:], accum_out=total[:]
        )
        inverse = keep.tile([P, 1], F32)
        nc.vector.reciprocal(out=inverse[:], in_=total[:])
        weights = keep.tile([P, 2, N], F32)
        nc.vector.tensor_scalar_mul(
            out=weights[:, :, : N // 2], in0=e[:].rearrange("p (a n) -> p a n", a=2), scalar1=inverse[:]
        )

        nc.sync.dma_start(
            out=out.rearrange("b (a n) o -> b a (n o)", a=2), in_=weights[0:1, :, : N // 2]
        )
